import numpy as np
import ml_dtypes


def mxq(x, axis, fmt="e4m3"):
    dtype, down = {"e4m3": (ml_dtypes.float8_e4m3fn, 7), "e5m2": (ml_dtypes.float8_e5m2, 14)}[fmt]
    v = np.moveaxis(np.asarray(x, np.float32).astype(ml_dtypes.bfloat16).astype(np.float64), axis, -1)
    blocks = v.reshape(v.shape[:-1] + (-1, 32))
    amax = np.abs(blocks).max(-1, keepdims=True)
    byte = np.maximum(np.where(amax > 0, np.frexp(amax)[1] - 1 + 127, 0) - down, 1)
    scale = np.exp2(byte - 127.0)
    codes = (blocks / scale).astype(np.float32).astype(dtype).astype(np.float64)
    return np.moveaxis((codes * scale).reshape(v.shape), -1, axis)


WIDE = False


def mx_kscale(k):
    if not WIDE:
        return np.ones(k)
    levels = np.array([10, -10, 5, -5, 0])
    if k % 512:
        return np.exp2(np.random.permutation(np.resize(levels, k // 32))).repeat(32)
    a = np.empty((k // 512, 16))
    for p in range(k // 512):
        a[p, :8] = np.random.permutation(np.resize(levels, 8))
        for g in range(8):
            far = levels[np.abs(levels - a[p, g]) >= 10]
            a[p, g + 8] = far[np.random.randint(len(far))]
    return np.exp2(a.ravel()).repeat(32)


BF16 = ml_dtypes.bfloat16


def bf(x):
    return np.asarray(x, np.float32).astype(BF16)


def f64(x):
    return np.asarray(x).astype(np.float64)


S, D, H, HD, CQ, CKV, O = 4096, 512, 6, 128, 96, 512, 2048
E = H * HD
ROPE_BASE = 10000.0


def rope(xh, cos, sin):
    half = xh.shape[-1] // 2
    x1, x2 = xh[..., :half], xh[..., half:]
    rot = np.concatenate([-x2, x1], axis=-1)
    return xh * cos[:, None, :] + rot * sin[:, None, :]


def setup_inputs():
    s, t = mx_kscale(D), mx_kscale(CKV)
    pos = np.arange(S, dtype=np.float64)[:, None]
    inv_freq = 1.0 / (ROPE_BASE ** (np.arange(0, HD, 2, dtype=np.float64) / HD))
    ang = pos * inv_freq[None, :]
    return {"x": bf(np.random.standard_normal((S, D)) * s[None, :]),
            "rope_cos": bf(np.concatenate([np.cos(ang), np.cos(ang)], axis=-1)),
            "rope_sin": bf(np.concatenate([np.sin(ang), np.sin(ang)], axis=-1)),
            "wkv_down": bf(np.random.standard_normal((CKV, D)) / np.sqrt(D) * t[:, None] / s[None, :]),
            "bkv_down": bf(np.random.standard_normal(CKV) * 0.3 * t),
            "wk_up": bf(np.random.standard_normal((E, CKV)) / np.sqrt(CKV) / t[None, :]),
            "bk_up": bf(np.random.standard_normal(E) * 0.3),
            "wv_up": bf(np.random.standard_normal((E, CKV)) / np.sqrt(CKV) / t[None, :]),
            "bv_up": bf(np.random.standard_normal(E) * 0.3)}


def reference(x, rope_cos, rope_sin, wkv_down, bkv_down, wk_up, bk_up, wv_up, bv_up):
    c_kv = (mxq(f64(x), 1, "e4m3") @ mxq(f64(wkv_down), 1, "e4m3").T) + f64(bkv_down)
    cq = mxq(c_kv, 1, "e4m3")
    k = ((cq @ mxq(f64(wk_up), 1, "e4m3").T) + f64(bk_up)).reshape(S, H, HD)
    v = ((cq @ mxq(f64(wv_up), 1, "e4m3").T) + f64(bv_up)).reshape(S, H, HD)
    return rope(k, f64(rope_cos), f64(rope_sin)), v

@@ -1,0 +1,339 @@
+from contextlib import ExitStack
+
+import concourse.mybir as mybir
+from concourse.masks import make_identity
+
+F32 = mybir.dt.float32
+BF16 = mybir.dt.bfloat16
+U32 = mybir.dt.uint32
+U8 = mybir.dt.uint8
+FP8X4 = mybir.dt.float8_e4m3fn_x4
+ADD = mybir.AluOpType.add
+MULT = mybir.AluOpType.mult
+IDENTITY = mybir.ActivationFunctionType.Identity
+
+P = 128
+TOKENS = 4096
+K = 512
+HEADS = 6
+HEAD = 128
+HALF = HEAD // 2
+E = HEADS * HEAD
+BANK = 512
+TILES = TOKENS // P
+BLOCK_TILES = 4
+BLOCK = BLOCK_TILES * P
+BLOCKS = TILES // BLOCK_TILES
+BLOCK_OUT = BLOCK_TILES * E
+
+FLOPS = 2 * TOKENS * K * (K + 2 * E)
+
+
+def tile_selfattention_pa_t_kernel(
+    tc, x, rope_cos, rope_sin, wkv_down, bkv_down, wk_up, bk_up, wv_up, bv_up, out_0, out_1
+):
+    nc = tc.nc
+    with ExitStack() as stack:
+        consts = stack.enter_context(tc.tile_pool(name="consts", bufs=1))
+        rows = stack.enter_context(tc.tile_pool(name="rows", bufs=1))
+        weights = stack.enter_context(tc.tile_pool(name="weights", bufs=1))
+        stage = stack.enter_context(tc.tile_pool(name="stage", bufs=3))
+        pairs = stack.enter_context(tc.tile_pool(name="pairs", bufs=2))
+        s_banks = stack.enter_context(tc.psum_pool(name="s_banks", bufs=4))
+        v_banks = stack.enter_context(tc.psum_pool(name="v_banks", bufs=4))
+        stack.enter_context(tc.manual_schedule())
+
+        x_dram = x.rearrange("(p t) d -> p t d", t=TILES)
+        cos_dram = rope_cos.rearrange("(p t) j -> p t j", t=TILES)
+        sin_dram = rope_sin.rearrange("(p t) j -> p t j", t=TILES)
+        k_dram = out_0.rearrange("(p t) h j -> p t (h j)", t=TILES)
+        v_dram = out_1.rearrange("(p t) h j -> p (t h j)", t=TILES)
+
+        x_rows = rows.tile([P, TILES, K], BF16)
+        cos_rows = rows.tile([P, TILES, HEAD], BF16)
+        sin_rows = rows.tile([P, TILES, HEAD], BF16)
+        sin_rot = rows.tile([P, TILES, HEAD], BF16)
+        down_rows = rows.tile([P, 4, K], BF16)
+        up_rows = rows.tile([P, 2 * HEADS, K], BF16)
+        bkv_bf = consts.tile([P, 4], BF16)
+        bk_bf = consts.tile([P, HEADS], BF16)
+        bv_bf = consts.tile([P, E], BF16)
+
+        def tiles_of(b):
+            return slice(b * BLOCK_TILES, (b + 1) * BLOCK_TILES)
+
+        def load_x(b):
+            nc.sync.dma_start(out=x_rows[:, tiles_of(b), :], in_=x_dram[:, tiles_of(b), :])
+
+        def load_rope(b):
+            nc.sync.dma_start(out=cos_rows[:, tiles_of(b), :], in_=cos_dram[:, tiles_of(b), :])
+            nc.sync.dma_start(out=sin_rows[:, tiles_of(b), :], in_=sin_dram[:, tiles_of(b), :])
+
+        nc.sync.dma_start(out=down_rows[:], in_=wkv_down.rearrange("(m t) d -> m t d", t=4))
+        load_x(0)
+        load_x(1)
+        nc.sync.dma_start(out=bkv_bf[:], in_=bkv_down.rearrange("(m t) -> m t", t=4))
+        nc.sync.dma_start(out=up_rows[:, 0:HEADS, :], in_=wk_up.rearrange("(a m) c -> m a c", m=P))
+        nc.sync.dma_start(
+            out=up_rows[:, HEADS : 2 * HEADS, :], in_=wv_up.rearrange("(a m) c -> m a c", m=P)
+        )
+        load_rope(0)
+        with nc.allow_non_contiguous_dma(reason="768 bias values, one head to a column"):
+            nc.sync.dma_start(out=bk_bf[:], in_=bk_up.rearrange("(h m) -> m h", m=P))
+        nc.sync.dma_start(out=bv_bf[:], in_=bv_up.partition_broadcast(P))
+        for b in range(2, BLOCKS):
+            load_x(b)
+            load_rope(b - 1)
+        load_rope(BLOCKS - 1)
+
+        ident_f32 = consts.tile([P, P], F32)
+        make_identity(nc, ident_f32[:])
+        ident_bf = consts.tile([P, P], BF16)
+        make_identity(nc, ident_bf[:])
+        swap_f32 = consts.tile([P, P], F32)
+        nc.vector.tensor_copy(out=swap_f32[:, 0:HALF], in_=ident_f32[:, HALF:HEAD])
+        nc.vector.tensor_copy(out=swap_f32[:, HALF:HEAD], in_=ident_f32[:, 0:HALF])
+        bkv_col = consts.tile([P, 4], F32)
+        bk_col = consts.tile([P, HEADS], F32)
+        bv_twice = consts.tile([P, 2, E], F32)
+        for b in range(BLOCKS):
+            nc.gpsimd.tensor_scalar(
+                out=sin_rot[:, tiles_of(b), 0:HALF], in0=sin_rows[:, tiles_of(b), HALF:HEAD],
+                scalar1=1.0, scalar2=0.0, op0=MULT, op1=ADD,
+            )
+            nc.gpsimd.tensor_scalar(
+                out=sin_rot[:, tiles_of(b), HALF:HEAD], in0=sin_rows[:, tiles_of(b), 0:HALF],
+                scalar1=-1.0, scalar2=0.0, op0=MULT, op1=ADD,
+            )
+            if b == 0:
+                nc.gpsimd.tensor_scalar(
+                    out=bv_twice[:], in0=bv_bf[:].unsqueeze(1).to_broadcast([P, 2, E]),
+                    scalar1=1.0, scalar2=0.0, op0=MULT, op1=ADD,
+                )
+
+        down_codes = weights.tile([P, K], U32, align_bytes=64)
+        down_scales = weights.tile([P, K], U8, align_bytes=64)
+        up_codes = weights.tile([P, 2 * E], U32, align_bytes=64)
+        up_scales = weights.tile([P, 2 * E], U8, align_bytes=64)
+
+        def words_to_partitions(four_tiles, banks, copy):
+            grouped = stage.tile([P, 4 * BLOCK], BF16, align_bytes=64)
+            words_in = four_tiles.bitcast(F32)
+            words_out = grouped[:].bitcast(F32).rearrange("p (r n u) -> p r n u", r=4, u=2)
+            for first in (0, 2):
+                bank = banks.tile([P, 2, 2, P], F32, tag="bank")
+                for r in range(2):
+                    for u in range(2):
+                        nc.tensor.transpose(
+                            bank[:, r, u, :], words_in[:, first + r, u : 2 * P : 2], ident_f32[:]
+                        )
+                copy(
+                    out=words_out[:, first : first + 2, :, :],
+                    in_=bank[:].rearrange("p r u n -> p r n u"),
+                )
+            return grouped
+
+        def quantise(grouped, codes, scales):
+            nc.vector.quantize_mx(out=codes.bitcast(FP8X4), scales=scales, in_=grouped[:])
+
+        x_grouped = {}
+        x_mx = {}
+        c_planes = {}
+        c_grouped = {}
+        c_mx = {}
+        tables = {}
+        products = {}
+        k_outs = {}
+
+        def x_words(b):
+            x_grouped[b] = words_to_partitions(x_rows[:, tiles_of(b), :], s_banks, nc.scalar.copy)
+
+        def x_quantise(b):
+            x_codes = pairs.tile([P, BLOCK], U32, align_bytes=64)
+            x_scales = pairs.tile([P, BLOCK], U8, align_bytes=64)
+            quantise(x_grouped[b], x_codes[:], x_scales[:])
+            x_mx[b] = (x_codes, x_scales)
+
+        def ckv_matmuls(b):
+            x_codes, x_scales = x_mx[b]
+            planes = pairs.tile([P, 4, BLOCK], BF16)
+            for t in range(4):
+                cols = slice(t * P, (t + 1) * P)
+                bank = s_banks.tile([P, BLOCK], F32, tag="bank")
+                nc.tensor.matmul_mx(
+                    out=bank[:],
+                    lhsT=down_codes[:, cols].bitcast(FP8X4),
+                    lhsT_scale=down_scales[:, cols],
+                    rhs=x_codes[:].bitcast(FP8X4),
+                    rhs_scale=x_scales[:],
+                    start=True,
+                    stop=True,
+                )
+                nc.scalar.activation(
+                    out=planes[:, t, :], in_=bank[:], func=IDENTITY, bias=bkv_col[:, t : t + 1], scale=1.0
+                )
+            c_planes[b] = planes
+
+        def ckv_regroup(b):
+            grouped = stage.tile([P, 4 * BLOCK], BF16, align_bytes=64)
+            nc.vector.tensor_copy(
+                out=grouped[:].rearrange("p (c i t) -> p c t i", i=4, t=4),
+                in_=c_planes[b][:].rearrange("p t (c i) -> p c t i", i=4),
+            )
+            c_grouped[b] = grouped
+
+        def ckv_quantise(b):
+            c_codes = pairs.tile([P, BLOCK], U32, align_bytes=64)
+            c_scales = pairs.tile([P, BLOCK], U8, align_bytes=64)
+            quantise(c_grouped[b], c_codes[:], c_scales[:])
+            c_mx[b] = (c_codes, c_scales)
+
+        def rope_tables(b):
+            bank = s_banks.tile([P, 2, BLOCK_TILES, P], BF16, tag="bank")
+            for i in range(BLOCK_TILES):
+                nc.tensor.transpose(bank[:, 0, i, :], cos_rows[:, b * BLOCK_TILES + i, :], ident_bf[:])
+                nc.tensor.transpose(bank[:, 1, i, :], sin_rot[:, b * BLOCK_TILES + i, :], ident_bf[:])
+            table = pairs.tile([P, 2, BLOCK], BF16)
+            nc.scalar.copy(out=table[:], in_=bank[:].rearrange("p w i n -> p w (i n)"))
+            tables[b] = table
+
+        def k_products(b, heads):
+            c_codes, c_scales = c_mx[b]
+            if b not in products:
+                product = pairs.tile([P, HEADS, 2, BLOCK], F32)
+                products[b] = product
+            product = products[b]
+            for h in heads:
+                cols = slice(h * HEAD, (h + 1) * HEAD)
+                bank = v_banks.tile([P, BLOCK], F32, tag="bank")
+                nc.tensor.matmul_mx(
+                    out=bank[:],
+                    lhsT=up_codes[:, cols].bitcast(FP8X4),
+                    lhsT_scale=up_scales[:, cols],
+                    rhs=c_codes[:].bitcast(FP8X4),
+                    rhs_scale=c_scales[:],
+                    start=True,
+                    stop=True,
+                )
+                nc.vector.scalar_tensor_tensor(
+                    out=product[:, h, :, :],
+                    in0=bank[:].unsqueeze(1).to_broadcast([P, 2, BLOCK]),
+                    scalar=bk_col[:, h : h + 1],
+                    in1=tables[b][:],
+                    op0=ADD,
+                    op1=MULT,
+                )
+
+        def k_back(b, heads):
+            product = products[b]
+            if b not in k_outs:
+                k_out = pairs.tile([P, BLOCK_TILES, HEADS, HEAD], F32)
+                k_outs[b] = k_out
+            k_out = k_outs[b]
+            for h in heads:
+                bank = s_banks.tile([P, BLOCK_TILES, HEAD], F32, tag="bank")
+                for i in range(BLOCK_TILES):
+                    toks = slice(i * P, (i + 1) * P)
+                    nc.tensor.matmul(
+                        out=bank[:, i, :], lhsT=product[:, h, 0, toks], rhs=ident_f32[:],
+                        is_transpose=True, start=True, stop=False,
+                    )
+                    nc.tensor.matmul(
+                        out=bank[:, i, :], lhsT=product[:, h, 1, toks], rhs=swap_f32[:],
+                        is_transpose=True, start=False, stop=True,
+                    )
+                nc.scalar.copy(out=k_out[:, :, h, :], in_=bank[:])
+            cols = slice(heads[0] * HEAD, (heads[-1] + 1) * HEAD)
+            nc.sync.dma_start(
+                out=k_dram[:, tiles_of(b), cols],
+                in_=k_out[:].rearrange("p i h j -> p i (h j)")[:, :, cols],
+            )
+
+        def v_block(b):
+            c_codes, c_scales = c_mx[b]
+            v_out = pairs.tile([P, BLOCK_OUT], F32)
+            bias = bv_twice[:].rearrange("p r e -> p (r e)")
+            for q in range(BLOCK_OUT // BANK):
+                on_vector = q % 3 == 0
+                bank = (v_banks if on_vector else s_banks).tile([P, BANK], F32, tag="bank")
+                col = q * BANK
+                while col < (q + 1) * BANK:
+                    i, e0 = divmod(col, E)
+                    width = min(E - e0, (q + 1) * BANK - col)
+                    toks = slice(i * P, (i + 1) * P)
+                    w_cols = slice(E + e0, E + e0 + width)
+                    nc.tensor.matmul_mx(
+                        out=bank[:, col - q * BANK : col - q * BANK + width],
+                        lhsT=c_codes[:, toks].bitcast(FP8X4),
+                        lhsT_scale=c_scales[:, toks],
+                        rhs=up_codes[:, w_cols].bitcast(FP8X4),
+                        rhs_scale=up_scales[:, w_cols],
+                        start=True,
+                        stop=True,
+                    )
+                    col += width
+                if on_vector:
+                    nc.vector.tensor_tensor(
+                        out=v_out[:, q * BANK : (q + 1) * BANK], in0=bank[:], in1=bias[:, 0:BANK], op=ADD
+                    )
+                else:
+                    nc.scalar.copy(out=v_out[:, q * BANK : (q + 1) * BANK], in_=bank[:])
+                if q % 3 == 2:
+                    two_banks = slice((q - 1) * BANK, (q + 1) * BANK)
+                    nc.gpsimd.tensor_tensor(
+                        out=v_out[:, two_banks], in0=v_out[:, two_banks], in1=bias[:, BANK : 3 * BANK], op=ADD
+                    )
+                    three_banks = slice((q - 2) * BANK, (q + 1) * BANK)
+                    nc.sync.dma_start(
+                        out=v_dram[:, b * BLOCK_OUT + (q - 2) * BANK : b * BLOCK_OUT + (q + 1) * BANK],
+                        in_=v_out[:, three_banks],
+                    )
+
+        def down_weights():
+            grouped = words_to_partitions(down_rows[:], v_banks, nc.vector.tensor_copy)
+            quantise(grouped, down_codes[:], down_scales[:])
+            nc.vector.tensor_copy(out=bkv_col[:], in_=bkv_bf[:])
+
+        def up_weights(chunk, banks, copy):
+            grouped = words_to_partitions(up_rows[:, 4 * chunk : 4 * chunk + 4, :], banks, copy)
+            cols = slice(chunk * BLOCK, (chunk + 1) * BLOCK)
+            quantise(grouped, up_codes[:, cols], up_scales[:, cols])
+
+        down_weights()
+        x_words(0)
+        x_quantise(0)
+        x_words(1)
+        up_weights(0, v_banks, nc.vector.tensor_copy)
+        ckv_matmuls(0)
+        up_weights(1, v_banks, nc.vector.tensor_copy)
+        ckv_regroup(0)
+        x_quantise(1)
+        ckv_quantise(0)
+        up_weights(2, s_banks, nc.scalar.copy)
+        nc.vector.tensor_copy(out=bk_col[:], in_=bk_bf[:])
+        rope_tables(0)
+        x_words(2)
+        ckv_matmuls(1)
+
+        first_heads = range(0, 4)
+        last_heads = range(4, HEADS)
+        for b in range(BLOCKS):
+            v_block(b)
+            k_products(b, first_heads)
+            if b + 1 < BLOCKS:
+                ckv_regroup(b + 1)
+            if b + 2 < BLOCKS:
+                x_quantise(b + 2)
+            if b + 1 < BLOCKS:
+                ckv_quantise(b + 1)
+            if b >= 1:
+                k_back(b - 1, last_heads)
+            if b + 1 < BLOCKS:
+                rope_tables(b + 1)
+            if b + 3 < BLOCKS:
+                x_words(b + 3)
+            k_back(b, first_heads)
+            k_products(b, last_heads)
+            if b + 2 < BLOCKS:
+                ckv_matmuls(b + 2)
+        k_back(BLOCKS - 1, last_heads)

@@ -19,12 +19,14 @@ HEADS = 6
 HEAD = 128
 HALF = HEAD // 2
 E = HEADS * HEAD
+T_HEADS = 4
+N_HEADS = HEADS - T_HEADS
+N_COLS = N_HEADS * HEAD
 BANK = 512
 TILES = TOKENS // P
 BLOCK_TILES = 4
 BLOCK = BLOCK_TILES * P
 BLOCKS = TILES // BLOCK_TILES
-BLOCK_OUT = BLOCK_TILES * E
 
 FLOPS = 2 * TOKENS * K * (K + 2 * E)
 
@@ -37,8 +39,9 @@ def tile_selfattention_pa_t_kernel(
         consts = stack.enter_context(tc.tile_pool(name="consts", bufs=1))
         rows = stack.enter_context(tc.tile_pool(name="rows", bufs=1))
         weights = stack.enter_context(tc.tile_pool(name="weights", bufs=1))
-        stage = stack.enter_context(tc.tile_pool(name="stage", bufs=3))
+        stage = stack.enter_context(tc.tile_pool(name="stage", bufs=2))
         pairs = stack.enter_context(tc.tile_pool(name="pairs", bufs=2))
+        triples = stack.enter_context(tc.tile_pool(name="triples", bufs=3))
         s_banks = stack.enter_context(tc.psum_pool(name="s_banks", bufs=4))
         v_banks = stack.enter_context(tc.psum_pool(name="v_banks", bufs=4))
         stack.enter_context(tc.manual_schedule())
@@ -47,7 +50,7 @@ def tile_selfattention_pa_t_kernel(
         cos_dram = rope_cos.rearrange("(p t) j -> p t j", t=TILES)
         sin_dram = rope_sin.rearrange("(p t) j -> p t j", t=TILES)
         k_dram = out_0.rearrange("(p t) h j -> p t (h j)", t=TILES)
-        v_dram = out_1.rearrange("(p t) h j -> p (t h j)", t=TILES)
+        v_dram = out_1.rearrange("(p t) h j -> p t (h j)", t=TILES)
 
         x_rows = rows.tile([P, TILES, K], BF16)
         cos_rows = rows.tile([P, TILES, HEAD], BF16)
@@ -56,8 +59,8 @@ def tile_selfattention_pa_t_kernel(
         down_rows = rows.tile([P, 4, K], BF16)
         up_rows = rows.tile([P, 2 * HEADS, K], BF16)
         bkv_bf = consts.tile([P, 4], BF16)
-        bk_bf = consts.tile([P, HEADS], BF16)
-        bv_bf = consts.tile([P, E], BF16)
+        bk_bf = consts.tile([P, T_HEADS], BF16)
+        row_bias = consts.tile([P, 2 * BANK], BF16)
 
         def tiles_of(b):
             return slice(b * BLOCK_TILES, (b + 1) * BLOCK_TILES)
@@ -71,16 +74,19 @@ def tile_selfattention_pa_t_kernel(
 
         nc.sync.dma_start(out=down_rows[:], in_=wkv_down.rearrange("(m t) d -> m t d", t=4))
         load_x(0)
-        load_x(1)
         nc.sync.dma_start(out=bkv_bf[:], in_=bkv_down.rearrange("(m t) -> m t", t=4))
-        nc.sync.dma_start(out=up_rows[:, 0:HEADS, :], in_=wk_up.rearrange("(a m) c -> m a c", m=P))
-        nc.sync.dma_start(
-            out=up_rows[:, HEADS : 2 * HEADS, :], in_=wv_up.rearrange("(a m) c -> m a c", m=P)
-        )
+        wk_rows = wk_up.rearrange("(a m) c -> m a c", m=P)
+        wv_rows = wv_up.rearrange("(a m) c -> m a c", m=P)
+        nc.sync.dma_start(out=up_rows[:, T_HEADS:HEADS, :], in_=wk_rows[:, T_HEADS:HEADS, :])
+        nc.sync.dma_start(out=up_rows[:, HEADS : HEADS + 2, :], in_=wv_rows[:, 0:2, :])
+        load_x(1)
+        with nc.allow_non_contiguous_dma(reason="512 bias values, one head to a column"):
+            nc.sync.dma_start(out=bk_bf[:], in_=bk_up[0 : T_HEADS * HEAD].rearrange("(h m) -> m h", m=P))
+        nc.sync.dma_start(out=row_bias[:, 0:N_COLS], in_=bk_up[T_HEADS * HEAD : E].partition_broadcast(P))
+        nc.sync.dma_start(out=row_bias[:, N_COLS : N_COLS + E], in_=bv_up.partition_broadcast(P))
+        nc.sync.dma_start(out=up_rows[:, HEADS + 2 : 2 * HEADS, :], in_=wv_rows[:, 2:HEADS, :])
         load_rope(0)
-        with nc.allow_non_contiguous_dma(reason="768 bias values, one head to a column"):
-            nc.sync.dma_start(out=bk_bf[:], in_=bk_up.rearrange("(h m) -> m h", m=P))
-        nc.sync.dma_start(out=bv_bf[:], in_=bv_up.partition_broadcast(P))
+        nc.sync.dma_start(out=up_rows[:, 0:T_HEADS, :], in_=wk_rows[:, 0:T_HEADS, :])
         for b in range(2, BLOCKS):
             load_x(b)
             load_rope(b - 1)
@@ -94,9 +100,9 @@ def tile_selfattention_pa_t_kernel(
         nc.vector.tensor_copy(out=swap_f32[:, 0:HALF], in_=ident_f32[:, HALF:HEAD])
         nc.vector.tensor_copy(out=swap_f32[:, HALF:HEAD], in_=ident_f32[:, 0:HALF])
         bkv_col = consts.tile([P, 4], F32)
-        bk_col = consts.tile([P, HEADS], F32)
-        bv_twice = consts.tile([P, 2, E], F32)
-        for b in range(BLOCKS):
+        bk_col = consts.tile([P, T_HEADS], F32)
+
+        def rotate_sin(b):
             nc.gpsimd.tensor_scalar(
                 out=sin_rot[:, tiles_of(b), 0:HALF], in0=sin_rows[:, tiles_of(b), HALF:HEAD],
                 scalar1=1.0, scalar2=0.0, op0=MULT, op1=ADD,
@@ -105,11 +111,6 @@ def tile_selfattention_pa_t_kernel(
                 out=sin_rot[:, tiles_of(b), HALF:HEAD], in0=sin_rows[:, tiles_of(b), 0:HALF],
                 scalar1=-1.0, scalar2=0.0, op0=MULT, op1=ADD,
             )
-            if b == 0:
-                nc.gpsimd.tensor_scalar(
-                    out=bv_twice[:], in0=bv_bf[:].unsqueeze(1).to_broadcast([P, 2, E]),
-                    scalar1=1.0, scalar2=0.0, op0=MULT, op1=ADD,
-                )
 
         down_codes = weights.tile([P, K], U32, align_bytes=64)
         down_scales = weights.tile([P, K], U8, align_bytes=64)
@@ -144,6 +145,7 @@ def tile_selfattention_pa_t_kernel(
         tables = {}
         products = {}
         k_outs = {}
+        row_outs = {}
 
         def x_words(b):
             x_grouped[b] = words_to_partitions(x_rows[:, tiles_of(b), :], s_banks, nc.scalar.copy)
@@ -174,9 +176,34 @@ def tile_selfattention_pa_t_kernel(
                 )
             c_planes[b] = planes
 
-        def ckv_regroup(b):
+        def ckv_direct(b):
+            x_codes, x_scales = x_mx[b]
             grouped = stage.tile([P, 4 * BLOCK], BF16, align_bytes=64)
-            nc.vector.tensor_copy(
+            for i in range(BLOCK_TILES):
+                toks = slice(i * P, (i + 1) * P)
+                bank = v_banks.tile([P, 4, P], F32, tag="bank")
+                for t in range(4):
+                    cols = slice(t * P, (t + 1) * P)
+                    nc.tensor.matmul_mx(
+                        out=bank[:, t, :],
+                        lhsT=down_codes[:, cols].bitcast(FP8X4),
+                        lhsT_scale=down_scales[:, cols],
+                        rhs=x_codes[:, toks].bitcast(FP8X4),
+                        rhs_scale=x_scales[:, toks],
+                        start=True,
+                        stop=True,
+                    )
+                nc.vector.tensor_tensor(
+                    out=grouped[:, 4 * i * P : 4 * (i + 1) * P].rearrange("p (n t) -> p n t", t=4),
+                    in0=bank[:].rearrange("p t n -> p n t"),
+                    in1=bkv_col[:].unsqueeze(1).to_broadcast([P, P, 4]),
+                    op=ADD,
+                )
+            c_grouped[b] = grouped
+
+        def ckv_regroup(b, copy):
+            grouped = stage.tile([P, 4 * BLOCK], BF16, align_bytes=64)
+            copy(
                 out=grouped[:].rearrange("p (c i t) -> p c t i", i=4, t=4),
                 in_=c_planes[b][:].rearrange("p t (c i) -> p c t i", i=4),
             )
@@ -197,10 +224,10 @@ def tile_selfattention_pa_t_kernel(
             nc.scalar.copy(out=table[:], in_=bank[:].rearrange("p w i n -> p w (i n)"))
             tables[b] = table
 
-        def k_products(b, heads):
+        def k_products(b, heads=range(T_HEADS)):
             c_codes, c_scales = c_mx[b]
             if b not in products:
-                product = pairs.tile([P, HEADS, 2, BLOCK], F32)
+                product = pairs.tile([P, T_HEADS, 2, BLOCK], F32)
                 products[b] = product
             product = products[b]
             for h in heads:
@@ -224,11 +251,8 @@ def tile_selfattention_pa_t_kernel(
                     op1=MULT,
                 )
 
-        def k_back(b, heads):
+        def k_back(b, heads=range(T_HEADS)):
             product = products[b]
-            if b not in k_outs:
-                k_out = pairs.tile([P, BLOCK_TILES, HEADS, HEAD], F32)
-                k_outs[b] = k_out
             k_out = k_outs[b]
             for h in heads:
                 bank = s_banks.tile([P, BLOCK_TILES, HEAD], F32, tag="bank")
@@ -243,97 +267,143 @@ def tile_selfattention_pa_t_kernel(
                         is_transpose=True, start=False, stop=True,
                     )
                 nc.scalar.copy(out=k_out[:, :, h, :], in_=bank[:])
+
+        def k_store(b, heads=range(HEADS)):
             cols = slice(heads[0] * HEAD, (heads[-1] + 1) * HEAD)
             nc.sync.dma_start(
                 out=k_dram[:, tiles_of(b), cols],
-                in_=k_out[:].rearrange("p i h j -> p i (h j)")[:, :, cols],
+                in_=k_outs[b][:].rearrange("p i h j -> p i (h j)")[:, :, cols],
             )
 
-        def v_block(b):
+        def rows_matmuls(b, part):
             c_codes, c_scales = c_mx[b]
-            v_out = pairs.tile([P, BLOCK_OUT], F32)
-            bias = bv_twice[:].rearrange("p r e -> p (r e)")
-            for q in range(BLOCK_OUT // BANK):
-                on_vector = q % 3 == 0
-                bank = (v_banks if on_vector else s_banks).tile([P, BANK], F32, tag="bank")
-                col = q * BANK
-                while col < (q + 1) * BANK:
-                    i, e0 = divmod(col, E)
-                    width = min(E - e0, (q + 1) * BANK - col)
-                    toks = slice(i * P, (i + 1) * P)
-                    w_cols = slice(E + e0, E + e0 + width)
-                    nc.tensor.matmul_mx(
-                        out=bank[:, col - q * BANK : col - q * BANK + width],
-                        lhsT=c_codes[:, toks].bitcast(FP8X4),
-                        lhsT_scale=c_scales[:, toks],
-                        rhs=up_codes[:, w_cols].bitcast(FP8X4),
-                        rhs_scale=up_scales[:, w_cols],
-                        start=True,
-                        stop=True,
-                    )
-                    col += width
-                if on_vector:
-                    nc.vector.tensor_tensor(
-                        out=v_out[:, q * BANK : (q + 1) * BANK], in0=bank[:], in1=bias[:, 0:BANK], op=ADD
-                    )
-                else:
-                    nc.scalar.copy(out=v_out[:, q * BANK : (q + 1) * BANK], in_=bank[:])
-                if q % 3 == 2:
-                    two_banks = slice((q - 1) * BANK, (q + 1) * BANK)
-                    nc.gpsimd.tensor_tensor(
-                        out=v_out[:, two_banks], in0=v_out[:, two_banks], in1=bias[:, BANK : 3 * BANK], op=ADD
-                    )
-                    three_banks = slice((q - 2) * BANK, (q + 1) * BANK)
-                    nc.sync.dma_start(
-                        out=v_dram[:, b * BLOCK_OUT + (q - 2) * BANK : b * BLOCK_OUT + (q + 1) * BANK],
-                        in_=v_out[:, three_banks],
-                    )
+            if b not in row_outs:
+                row_out = pairs.tile([P, BLOCK_TILES, 2 * BANK], F32)
+                row_outs[b] = row_out
+            row_out = row_outs[b]
+            w_cols = slice((1 + part) * BANK, (2 + part) * BANK)
+            o_cols = slice(part * BANK, (part + 1) * BANK)
+            for i in range(BLOCK_TILES):
+                toks = slice(i * P, (i + 1) * P)
+                bank = v_banks.tile([P, BANK], F32, tag="bank")
+                nc.tensor.matmul_mx(
+                    out=bank[:],
+                    lhsT=c_codes[:, toks].bitcast(FP8X4),
+                    lhsT_scale=c_scales[:, toks],
+                    rhs=up_codes[:, w_cols].bitcast(FP8X4),
+                    rhs_scale=up_scales[:, w_cols],
+                    start=True,
+                    stop=True,
+                )
+                nc.vector.tensor_tensor(out=row_out[:, i, o_cols], in0=bank[:], in1=row_bias[:, o_cols], op=ADD)
+
+        def v_store(b):
+            nc.sync.dma_start(
+                out=v_dram[:, tiles_of(b), :], in_=row_outs[b][:, :, N_COLS : N_COLS + E]
+            )
+
+        def rope_rows(b):
+            k_out = triples.tile([P, BLOCK_TILES, HEADS, HEAD], F32)
+            k_outs[b] = k_out
+            for first in range(0, BLOCK_TILES, 2):
+                here = slice(first, first + 2)
+                toks = slice(b * BLOCK_TILES + first, b * BLOCK_TILES + first + 2)
+                k_in = row_outs[b][:, here, 0:N_COLS].rearrange("p i (h j) -> p i h j", j=HEAD)
+                out = k_out[:, here, T_HEADS:HEADS, :]
+                cos = cos_rows[:, toks, :].unsqueeze(2).to_broadcast([P, 2, N_HEADS, HEAD])
+                sin = sin_rot[:, toks, :].unsqueeze(2).to_broadcast([P, 2, N_HEADS, HEAD])
+                nc.gpsimd.tensor_tensor(out=out, in0=k_in, in1=cos, op=MULT)
+                nc.gpsimd.tensor_tensor(out=k_in, in0=k_in, in1=sin, op=MULT)
+                nc.gpsimd.tensor_tensor(
+                    out=out[:, :, :, 0:HALF], in0=out[:, :, :, 0:HALF], in1=k_in[:, :, :, HALF:HEAD], op=ADD
+                )
+                nc.gpsimd.tensor_tensor(
+                    out=out[:, :, :, HALF:HEAD], in0=out[:, :, :, HALF:HEAD], in1=k_in[:, :, :, 0:HALF], op=ADD
+                )
 
         def down_weights():
             grouped = words_to_partitions(down_rows[:], v_banks, nc.vector.tensor_copy)
             quantise(grouped, down_codes[:], down_scales[:])
             nc.vector.tensor_copy(out=bkv_col[:], in_=bkv_bf[:])
 
-        def up_weights(chunk, banks, copy):
-            grouped = words_to_partitions(up_rows[:, 4 * chunk : 4 * chunk + 4, :], banks, copy)
-            cols = slice(chunk * BLOCK, (chunk + 1) * BLOCK)
-            quantise(grouped, up_codes[:, cols], up_scales[:, cols])
+        up_grouped = {}
 
+        def up_words(chunk):
+            rows_here = up_rows[:, 4 * chunk : 4 * chunk + 4, :]
+            up_grouped[chunk] = words_to_partitions(rows_here, s_banks, nc.scalar.copy)
+
+        def up_quantise(chunk):
+            cols = slice(chunk * BLOCK, (chunk + 1) * BLOCK)
+            quantise(up_grouped[chunk], up_codes[:, cols], up_scales[:, cols])
+
+        rotate_sin(0)
+        rotate_sin(1)
         down_weights()
         x_words(0)
         x_quantise(0)
-        x_words(1)
-        up_weights(0, v_banks, nc.vector.tensor_copy)
-        ckv_matmuls(0)
-        up_weights(1, v_banks, nc.vector.tensor_copy)
-        ckv_regroup(0)
-        x_quantise(1)
+        up_words(1)
+        ckv_direct(0)
+        up_quantise(1)
         ckv_quantise(0)
-        up_weights(2, s_banks, nc.scalar.copy)
-        nc.vector.tensor_copy(out=bk_col[:], in_=bk_bf[:])
-        rope_tables(0)
-        x_words(2)
+        x_words(1)
+        rows_matmuls(0, 0)
+        rope_rows(0)
+        up_words(2)
+        x_quantise(1)
+        up_quantise(2)
         ckv_matmuls(1)
+        rows_matmuls(0, 1)
+        v_store(0)
+        up_words(0)
+        rope_tables(0)
+        ckv_regroup(1, nc.vector.tensor_copy)
+        up_quantise(0)
+        nc.vector.tensor_copy(out=bk_col[:], in_=bk_bf[:])
+        x_words(2)
+        k_products(0)
+        rotate_sin(2)
+        rope_tables(1)
+        x_quantise(2)
+        ckv_quantise(1)
+        x_words(3)
 
-        first_heads = range(0, 4)
-        last_heads = range(4, HEADS)
-        for b in range(BLOCKS):
-            v_block(b)
-            k_products(b, first_heads)
-            if b + 1 < BLOCKS:
-                ckv_regroup(b + 1)
-            if b + 2 < BLOCKS:
-                x_quantise(b + 2)
-            if b + 1 < BLOCKS:
+        for b in range(1, BLOCKS):
+            last = b == BLOCKS - 1
+            if not last:
+                if b + 2 < BLOCKS:
+                    x_quantise(b + 2)
+                rows_matmuls(b, 0)
+                rope_rows(b)
+                for ahead in (2, 3) if b == 1 else (b + 2,):
+                    if ahead < BLOCKS:
+                        ckv_matmuls(ahead)
+                        if ahead == 2:
+                            ckv_regroup(2, nc.scalar.copy)
+            rows_matmuls(b, 1)
+            v_store(b)
+            if b + 2 == BLOCKS:
                 ckv_quantise(b + 1)
-            if b >= 1:
-                k_back(b - 1, last_heads)
-            if b + 1 < BLOCKS:
+                rows_matmuls(b + 1, 0)
+                rope_rows(b + 1)
+            if last:
+                k_products(b)
+                k_back(b - 1)
+                k_store(b - 1)
+                k_back(b, range(0, 2))
+                k_store(b, range(T_HEADS, HEADS))
+                k_store(b, range(0, 2))
+                k_back(b, range(2, 4))
+                k_store(b, range(2, 4))
+            else:
+                k_products(b)
+                if b + 2 < BLOCKS:
+                    ckv_regroup(b + 2, nc.scalar.copy)
+                if b + 2 < BLOCKS:
+                    rotate_sin(b + 2)
+                if b + 3 < BLOCKS:
+                    x_words(b + 3)
                 rope_tables(b + 1)
-            if b + 3 < BLOCKS:
-                x_words(b + 3)
-            k_back(b, first_heads)
-            k_products(b, last_heads)
-            if b + 2 < BLOCKS:
-                ckv_matmuls(b + 2)
-        k_back(BLOCKS - 1, last_heads)
+                if b + 2 < BLOCKS:
+                    ckv_quantise(b + 1)
+                k_back(b - 1)
+                k_store(b - 1)

@@ -19,14 +19,15 @@ HEADS = 6
 HEAD = 128
 HALF = HEAD // 2
 E = HEADS * HEAD
-T_HEADS = 4
-N_HEADS = HEADS - T_HEADS
-N_COLS = N_HEADS * HEAD
+T_HEADS = 5
 BANK = 512
 TILES = TOKENS // P
 BLOCK_TILES = 4
 BLOCK = BLOCK_TILES * P
 BLOCKS = TILES // BLOCK_TILES
+BLOCK_OUT = BLOCK_TILES * E
+
+BY_SCALAR = (1, 4)
 
 FLOPS = 2 * TOKENS * K * (K + 2 * E)
 
@@ -39,18 +40,19 @@ def tile_selfattention_pa_t_kernel(
         consts = stack.enter_context(tc.tile_pool(name="consts", bufs=1))
         rows = stack.enter_context(tc.tile_pool(name="rows", bufs=1))
         weights = stack.enter_context(tc.tile_pool(name="weights", bufs=1))
-        stage = stack.enter_context(tc.tile_pool(name="stage", bufs=2))
+        x_stage = stack.enter_context(tc.tile_pool(name="x_stage", bufs=3))
+        c_stage = stack.enter_context(tc.tile_pool(name="c_stage", bufs=2))
         pairs = stack.enter_context(tc.tile_pool(name="pairs", bufs=2))
         triples = stack.enter_context(tc.tile_pool(name="triples", bufs=3))
-        s_banks = stack.enter_context(tc.psum_pool(name="s_banks", bufs=4))
-        v_banks = stack.enter_context(tc.psum_pool(name="v_banks", bufs=4))
+        s_banks = stack.enter_context(tc.psum_pool(name="s_banks", bufs=3))
+        v_banks = stack.enter_context(tc.psum_pool(name="v_banks", bufs=5))
         stack.enter_context(tc.manual_schedule())
 
         x_dram = x.rearrange("(p t) d -> p t d", t=TILES)
         cos_dram = rope_cos.rearrange("(p t) j -> p t j", t=TILES)
         sin_dram = rope_sin.rearrange("(p t) j -> p t j", t=TILES)
         k_dram = out_0.rearrange("(p t) h j -> p t (h j)", t=TILES)
-        v_dram = out_1.rearrange("(p t) h j -> p t (h j)", t=TILES)
+        v_dram = out_1.rearrange("(p t) h j -> p (t h j)", t=TILES)
 
         x_rows = rows.tile([P, TILES, K], BF16)
         cos_rows = rows.tile([P, TILES, HEAD], BF16)
@@ -60,7 +62,8 @@ def tile_selfattention_pa_t_kernel(
         up_rows = rows.tile([P, 2 * HEADS, K], BF16)
         bkv_bf = consts.tile([P, 4], BF16)
         bk_bf = consts.tile([P, T_HEADS], BF16)
-        row_bias = consts.tile([P, 2 * BANK], BF16)
+        bk_row = consts.tile([P, HEAD], BF16)
+        bv_row = consts.tile([P, 2, E], BF16)
 
         def tiles_of(b):
             return slice(b * BLOCK_TILES, (b + 1) * BLOCK_TILES)
@@ -77,16 +80,16 @@ def tile_selfattention_pa_t_kernel(
         nc.sync.dma_start(out=bkv_bf[:], in_=bkv_down.rearrange("(m t) -> m t", t=4))
         wk_rows = wk_up.rearrange("(a m) c -> m a c", m=P)
         wv_rows = wv_up.rearrange("(a m) c -> m a c", m=P)
-        nc.sync.dma_start(out=up_rows[:, T_HEADS:HEADS, :], in_=wk_rows[:, T_HEADS:HEADS, :])
+        nc.sync.dma_start(out=up_rows[:, 4:HEADS, :], in_=wk_rows[:, 4:HEADS, :])
         nc.sync.dma_start(out=up_rows[:, HEADS : HEADS + 2, :], in_=wv_rows[:, 0:2, :])
-        load_x(1)
-        with nc.allow_non_contiguous_dma(reason="512 bias values, one head to a column"):
-            nc.sync.dma_start(out=bk_bf[:], in_=bk_up[0 : T_HEADS * HEAD].rearrange("(h m) -> m h", m=P))
-        nc.sync.dma_start(out=row_bias[:, 0:N_COLS], in_=bk_up[T_HEADS * HEAD : E].partition_broadcast(P))
-        nc.sync.dma_start(out=row_bias[:, N_COLS : N_COLS + E], in_=bv_up.partition_broadcast(P))
         nc.sync.dma_start(out=up_rows[:, HEADS + 2 : 2 * HEADS, :], in_=wv_rows[:, 2:HEADS, :])
+        load_x(1)
+        nc.sync.dma_start(out=bk_row[:], in_=bk_up[T_HEADS * HEAD : E].partition_broadcast(P))
+        nc.sync.dma_start(out=bv_row[:, 0, :], in_=bv_up.partition_broadcast(P))
+        with nc.allow_non_contiguous_dma(reason="640 bias values, one head to a column"):
+            nc.sync.dma_start(out=bk_bf[:], in_=bk_up[0 : T_HEADS * HEAD].rearrange("(h m) -> m h", m=P))
         load_rope(0)
-        nc.sync.dma_start(out=up_rows[:, 0:T_HEADS, :], in_=wk_rows[:, 0:T_HEADS, :])
+        nc.sync.dma_start(out=up_rows[:, 0:4, :], in_=wk_rows[:, 0:4, :])
         for b in range(2, BLOCKS):
             load_x(b)
             load_rope(b - 1)
@@ -118,7 +121,7 @@ def tile_selfattention_pa_t_kernel(
         up_scales = weights.tile([P, 2 * E], U8, align_bytes=64)
 
         def words_to_partitions(four_tiles, banks, copy):
-            grouped = stage.tile([P, 4 * BLOCK], BF16, align_bytes=64)
+            grouped = x_stage.tile([P, 4 * BLOCK], BF16, align_bytes=64)
             words_in = four_tiles.bitcast(F32)
             words_out = grouped[:].bitcast(F32).rearrange("p (r n u) -> p r n u", r=4, u=2)
             for first in (0, 2):
@@ -144,8 +147,10 @@ def tile_selfattention_pa_t_kernel(
         c_mx = {}
         tables = {}
         products = {}
+        k_banks = {}
         k_outs = {}
-        row_outs = {}
+        k_in = {}
+        v_outs = {}
 
         def x_words(b):
             x_grouped[b] = words_to_partitions(x_rows[:, tiles_of(b), :], s_banks, nc.scalar.copy)
@@ -156,10 +161,13 @@ def tile_selfattention_pa_t_kernel(
             quantise(x_grouped[b], x_codes[:], x_scales[:])
             x_mx[b] = (x_codes, x_scales)
 
-        def ckv_matmuls(b):
+        def ckv_matmuls(b, parts=range(4)):
             x_codes, x_scales = x_mx[b]
-            planes = pairs.tile([P, 4, BLOCK], BF16)
-            for t in range(4):
+            if b not in c_planes:
+                planes = pairs.tile([P, 4, BLOCK], BF16)
+                c_planes[b] = planes
+            planes = c_planes[b]
+            for t in parts:
                 cols = slice(t * P, (t + 1) * P)
                 bank = s_banks.tile([P, BLOCK], F32, tag="bank")
                 nc.tensor.matmul_mx(
@@ -174,11 +182,10 @@ def tile_selfattention_pa_t_kernel(
                 nc.scalar.activation(
                     out=planes[:, t, :], in_=bank[:], func=IDENTITY, bias=bkv_col[:, t : t + 1], scale=1.0
                 )
-            c_planes[b] = planes
 
         def ckv_direct(b):
             x_codes, x_scales = x_mx[b]
-            grouped = stage.tile([P, 4 * BLOCK], BF16, align_bytes=64)
+            grouped = c_stage.tile([P, 4 * BLOCK], BF16, align_bytes=64)
             for i in range(BLOCK_TILES):
                 toks = slice(i * P, (i + 1) * P)
                 bank = v_banks.tile([P, 4, P], F32, tag="bank")
@@ -201,11 +208,16 @@ def tile_selfattention_pa_t_kernel(
                 )
             c_grouped[b] = grouped
 
-        def ckv_regroup(b, copy):
-            grouped = stage.tile([P, 4 * BLOCK], BF16, align_bytes=64)
-            copy(
-                out=grouped[:].rearrange("p (c i t) -> p c t i", i=4, t=4),
-                in_=c_planes[b][:].rearrange("p t (c i) -> p c t i", i=4),
+        def ckv_regroup(b):
+            grouped = c_stage.tile([P, 4 * BLOCK], BF16, align_bytes=64)
+            words = grouped[:].rearrange("p (c i t) -> p c t i", i=4, t=4)
+            planes = c_planes[b][:].rearrange("p t (c i) -> p c t i", i=4)
+            half = BLOCK // 8
+            nc.scalar.copy(out=words[:, 0:half], in_=planes[:, 0:half])
+            nc.gpsimd.tensor_scalar(
+                out=grouped[:].rearrange("p (n t) -> p n t", t=4)[:, BLOCK // 2 : BLOCK, :],
+                in0=c_planes[b][:].rearrange("p t n -> p n t")[:, BLOCK // 2 : BLOCK, :],
+                scalar1=1.0, scalar2=0.0, op0=MULT, op1=ADD,
             )
             c_grouped[b] = grouped
 
@@ -224,13 +236,10 @@ def tile_selfattention_pa_t_kernel(
             nc.scalar.copy(out=table[:], in_=bank[:].rearrange("p w i n -> p w (i n)"))
             tables[b] = table
 
-        def k_products(b, heads=range(T_HEADS)):
+        def k_matmuls(b):
             c_codes, c_scales = c_mx[b]
-            if b not in products:
-                product = pairs.tile([P, T_HEADS, 2, BLOCK], F32)
-                products[b] = product
-            product = products[b]
-            for h in heads:
+            k_banks[b] = []
+            for h in range(T_HEADS):
                 cols = slice(h * HEAD, (h + 1) * HEAD)
                 bank = v_banks.tile([P, BLOCK], F32, tag="bank")
                 nc.tensor.matmul_mx(
@@ -242,9 +251,17 @@ def tile_selfattention_pa_t_kernel(
                     start=True,
                     stop=True,
                 )
+                k_banks[b].append(bank)
+
+        def k_products(b, heads=range(T_HEADS)):
+            if b not in products:
+                product = pairs.tile([P, T_HEADS, 2, BLOCK], F32)
+                products[b] = product
+            product = products[b]
+            for h in heads:
                 nc.vector.scalar_tensor_tensor(
                     out=product[:, h, :, :],
-                    in0=bank[:].unsqueeze(1).to_broadcast([P, 2, BLOCK]),
+                    in0=k_banks[b][h][:].unsqueeze(1).to_broadcast([P, 2, BLOCK]),
                     scalar=bk_col[:, h : h + 1],
                     in1=tables[b][:],
                     op0=ADD,
@@ -275,19 +292,14 @@ def tile_selfattention_pa_t_kernel(
                 in_=k_outs[b][:].rearrange("p i h j -> p i (h j)")[:, :, cols],
             )
 
-        def rows_matmuls(b, part):
+        def k_rows(b):
             c_codes, c_scales = c_mx[b]
-            if b not in row_outs:
-                row_out = pairs.tile([P, BLOCK_TILES, 2 * BANK], F32)
-                row_outs[b] = row_out
-            row_out = row_outs[b]
-            w_cols = slice((1 + part) * BANK, (2 + part) * BANK)
-            o_cols = slice(part * BANK, (part + 1) * BANK)
+            w_cols = slice(T_HEADS * HEAD, E)
+            bank = v_banks.tile([P, BLOCK_TILES, HEAD], F32, tag="bank")
             for i in range(BLOCK_TILES):
                 toks = slice(i * P, (i + 1) * P)
-                bank = v_banks.tile([P, BANK], F32, tag="bank")
                 nc.tensor.matmul_mx(
-                    out=bank[:],
+                    out=bank[:, i, :],
                     lhsT=c_codes[:, toks].bitcast(FP8X4),
                     lhsT_scale=c_scales[:, toks],
                     rhs=up_codes[:, w_cols].bitcast(FP8X4),
@@ -295,31 +307,66 @@ def tile_selfattention_pa_t_kernel(
                     start=True,
                     stop=True,
                 )
-                nc.vector.tensor_tensor(out=row_out[:, i, o_cols], in0=bank[:], in1=row_bias[:, o_cols], op=ADD)
-
-        def v_store(b):
-            nc.sync.dma_start(
-                out=v_dram[:, tiles_of(b), :], in_=row_outs[b][:, :, N_COLS : N_COLS + E]
+            k_row = pairs.tile([P, BLOCK_TILES, HEAD], F32)
+            nc.vector.tensor_tensor(
+                out=k_row[:], in0=bank[:], in1=bk_row[:].unsqueeze(1).to_broadcast([P, BLOCK_TILES, HEAD]), op=ADD
             )
+            k_in[b] = k_row
 
         def rope_rows(b):
             k_out = triples.tile([P, BLOCK_TILES, HEADS, HEAD], F32)
             k_outs[b] = k_out
-            for first in range(0, BLOCK_TILES, 2):
-                here = slice(first, first + 2)
-                toks = slice(b * BLOCK_TILES + first, b * BLOCK_TILES + first + 2)
-                k_in = row_outs[b][:, here, 0:N_COLS].rearrange("p i (h j) -> p i h j", j=HEAD)
-                out = k_out[:, here, T_HEADS:HEADS, :]
-                cos = cos_rows[:, toks, :].unsqueeze(2).to_broadcast([P, 2, N_HEADS, HEAD])
-                sin = sin_rot[:, toks, :].unsqueeze(2).to_broadcast([P, 2, N_HEADS, HEAD])
-                nc.gpsimd.tensor_tensor(out=out, in0=k_in, in1=cos, op=MULT)
-                nc.gpsimd.tensor_tensor(out=k_in, in0=k_in, in1=sin, op=MULT)
-                nc.gpsimd.tensor_tensor(
-                    out=out[:, :, :, 0:HALF], in0=out[:, :, :, 0:HALF], in1=k_in[:, :, :, HALF:HEAD], op=ADD
-                )
-                nc.gpsimd.tensor_tensor(
-                    out=out[:, :, :, HALF:HEAD], in0=out[:, :, :, HALF:HEAD], in1=k_in[:, :, :, 0:HALF], op=ADD
-                )
+            k_row = k_in[b]
+            out = k_out[:, :, T_HEADS, :]
+            nc.gpsimd.tensor_tensor(out=out, in0=k_row[:], in1=cos_rows[:, tiles_of(b), :], op=MULT)
+            nc.gpsimd.tensor_tensor(out=k_row[:], in0=k_row[:], in1=sin_rot[:, tiles_of(b), :], op=MULT)
+            nc.gpsimd.tensor_tensor(
+                out=out[:, :, 0:HALF], in0=out[:, :, 0:HALF], in1=k_row[:, :, HALF:HEAD], op=ADD
+            )
+            nc.gpsimd.tensor_tensor(
+                out=out[:, :, HALF:HEAD], in0=out[:, :, HALF:HEAD], in1=k_row[:, :, 0:HALF], op=ADD
+            )
+
+        def v_banks_of(b, banks_here):
+            c_codes, c_scales = c_mx[b]
+            if b not in v_outs:
+                v_out = pairs.tile([P, BLOCK_OUT], F32)
+                v_outs[b] = v_out
+            v_out = v_outs[b]
+            bias = bv_row[:].rearrange("p r e -> p (r e)")
+            for q in banks_here:
+                by_scalar = q in BY_SCALAR and b < BLOCKS - 1
+                bank = (s_banks if by_scalar else v_banks).tile([P, BANK], F32, tag="bank")
+                col = q * BANK
+                while col < (q + 1) * BANK:
+                    i, e0 = divmod(col, E)
+                    width = min(E - e0, (q + 1) * BANK - col)
+                    toks = slice(i * P, (i + 1) * P)
+                    w_cols = slice(E + e0, E + e0 + width)
+                    nc.tensor.matmul_mx(
+                        out=bank[:, col - q * BANK : col - q * BANK + width],
+                        lhsT=c_codes[:, toks].bitcast(FP8X4),
+                        lhsT_scale=c_scales[:, toks],
+                        rhs=up_codes[:, w_cols].bitcast(FP8X4),
+                        rhs_scale=up_scales[:, w_cols],
+                        start=True,
+                        stop=True,
+                    )
+                    col += width
+                o_cols = slice(q * BANK, (q + 1) * BANK)
+                first = q * BANK % E
+                b_cols = slice(first, first + BANK)
+                if by_scalar:
+                    nc.scalar.copy(out=v_out[:, o_cols], in_=bank[:])
+                    nc.gpsimd.tensor_tensor(out=v_out[:, o_cols], in0=v_out[:, o_cols], in1=bias[:, b_cols], op=ADD)
+                else:
+                    nc.vector.tensor_tensor(out=v_out[:, o_cols], in0=bank[:], in1=bias[:, b_cols], op=ADD)
+
+        def v_store(b, half):
+            cols = slice(half * BLOCK_OUT // 2, (half + 1) * BLOCK_OUT // 2)
+            nc.sync.dma_start(
+                out=v_dram[:, b * BLOCK_OUT + cols.start : b * BLOCK_OUT + cols.stop], in_=v_outs[b][:, cols]
+            )
 
         def down_weights():
             grouped = words_to_partitions(down_rows[:], v_banks, nc.vector.tensor_copy)
@@ -336,74 +383,100 @@ def tile_selfattention_pa_t_kernel(
             cols = slice(chunk * BLOCK, (chunk + 1) * BLOCK)
             quantise(up_grouped[chunk], up_codes[:, cols], up_scales[:, cols])
 
-        rotate_sin(0)
-        rotate_sin(1)
         down_weights()
         x_words(0)
-        x_quantise(0)
         up_words(1)
-        ckv_direct(0)
+        rotate_sin(0)
+        x_quantise(0)
         up_quantise(1)
+        ckv_direct(0)
+        up_words(2)
         ckv_quantise(0)
         x_words(1)
-        rows_matmuls(0, 0)
-        rope_rows(0)
-        up_words(2)
-        x_quantise(1)
         up_quantise(2)
-        ckv_matmuls(1)
-        rows_matmuls(0, 1)
-        v_store(0)
+        x_quantise(1)
+        nc.gpsimd.tensor_scalar(
+            out=bv_row[:, 1, :], in0=bv_row[:, 0, :], scalar1=1.0, scalar2=0.0, op0=MULT, op1=ADD
+        )
+        k_rows(0)
+        rope_rows(0)
+        for q in (0, 2, 3, 5):
+            v_banks_of(0, [q])
+        rotate_sin(1)
         up_words(0)
-        rope_tables(0)
-        ckv_regroup(1, nc.vector.tensor_copy)
         up_quantise(0)
-        nc.vector.tensor_copy(out=bk_col[:], in_=bk_bf[:])
+        rope_tables(0)
+        ckv_direct(1)
         x_words(2)
-        k_products(0)
-        rotate_sin(2)
-        rope_tables(1)
-        x_quantise(2)
-        ckv_quantise(1)
+        nc.vector.tensor_copy(out=bk_col[:], in_=bk_bf[:])
+        k_matmuls(0)
+        v_banks_of(0, [4])
         x_words(3)
+        v_banks_of(0, [1])
+        v_store(0, 0)
+        v_store(0, 1)
+        x_quantise(2)
+        k_products(0, [0])
+        ckv_matmuls(2, [0, 1])
+        k_products(0, [1])
+        ckv_quantise(1)
+        ckv_matmuls(2, [2, 3])
+        k_products(0, [2])
+        x_quantise(3)
+        rotate_sin(2)
+        ckv_regroup(2)
+        rope_tables(1)
+        k_products(0, [3, 4])
+        ckv_quantise(2)
 
-        for b in range(1, BLOCKS):
-            last = b == BLOCKS - 1
-            if not last:
-                if b + 2 < BLOCKS:
-                    x_quantise(b + 2)
-                rows_matmuls(b, 0)
-                rope_rows(b)
-                for ahead in (2, 3) if b == 1 else (b + 2,):
-                    if ahead < BLOCKS:
-                        ckv_matmuls(ahead)
-                        if ahead == 2:
-                            ckv_regroup(2, nc.scalar.copy)
-            rows_matmuls(b, 1)
-            v_store(b)
-            if b + 2 == BLOCKS:
-                ckv_quantise(b + 1)
-                rows_matmuls(b + 1, 0)
-                rope_rows(b + 1)
-            if last:
-                k_products(b)
-                k_back(b - 1)
-                k_store(b - 1)
-                k_back(b, range(0, 2))
-                k_store(b, range(T_HEADS, HEADS))
-                k_store(b, range(0, 2))
-                k_back(b, range(2, 4))
-                k_store(b, range(2, 4))
-            else:
-                k_products(b)
-                if b + 2 < BLOCKS:
-                    ckv_regroup(b + 2, nc.scalar.copy)
-                if b + 2 < BLOCKS:
-                    rotate_sin(b + 2)
-                if b + 3 < BLOCKS:
-                    x_words(b + 3)
-                rope_tables(b + 1)
-                if b + 2 < BLOCKS:
-                    ckv_quantise(b + 1)
-                k_back(b - 1)
-                k_store(b - 1)
+        for b in range(1, BLOCKS - 1):
+            v_banks_of(b, [1])
+            k_rows(b)
+            v_banks_of(b, [0])
+            if b + 2 < BLOCKS:
+                ckv_matmuls(b + 2, [0, 1])
+            rope_rows(b)
+            v_banks_of(b, [2])
+            v_store(b, 0)
+            v_banks_of(b, [3])
+            if b + 2 < BLOCKS:
+                ckv_matmuls(b + 2, [2])
+            v_banks_of(b, [5])
+            if b + 2 < BLOCKS:
+                ckv_matmuls(b + 2, [3])
+            v_banks_of(b, [4])
+            v_store(b, 1)
+            k_matmuls(b)
+            if b + 2 < BLOCKS:
+                ckv_regroup(b + 2)
+            k_products(b)
+            if b + 2 < BLOCKS:
+                rotate_sin(b + 2)
+            if b + 3 < BLOCKS:
+                x_words(b + 3)
+            k_back(b - 1, [0])
+            rope_tables(b + 1)
+            k_back(b - 1, [1, 2, 3, 4])
+            k_store(b - 1)
+            if b + 3 < BLOCKS:
+                x_quantise(b + 3)
+            if b + 2 < BLOCKS:
+                ckv_quantise(b + 2)
+
+        last = BLOCKS - 1
+        for q in range(6):
+            v_banks_of(last, [q])
+        v_store(last, 0)
+        v_store(last, 1)
+        k_rows(last)
+        rope_rows(last)
+        k_back(last - 1, [0, 1, 2])
+        k_matmuls(last)
+        k_back(last - 1, [3, 4])
+        k_store(last - 1)
+        k_products(last, [0, 1])
+        k_back(last, [0, 1])
+        k_store(last, range(0, 2))
+        k_products(last, [2, 3, 4])
+        k_back(last, [2, 3, 4])
+        k_store(last, range(2, HEADS))

@@ -210,13 +210,12 @@ def tile_selfattention_pa_t_kernel(
 
         def ckv_regroup(b):
             grouped = c_stage.tile([P, 4 * BLOCK], BF16, align_bytes=64)
-            words = grouped[:].rearrange("p (c i t) -> p c t i", i=4, t=4)
-            planes = c_planes[b][:].rearrange("p t (c i) -> p c t i", i=4)
-            half = BLOCK // 8
-            nc.scalar.copy(out=words[:, 0:half], in_=planes[:, 0:half])
+            words = grouped[:].rearrange("p (n t) -> p n t", t=4)
+            planes = c_planes[b][:].rearrange("p t n -> p n t")
+            half = BLOCK // 2
+            nc.scalar.copy(out=words[:, 0:half, :], in_=planes[:, 0:half, :])
             nc.gpsimd.tensor_scalar(
-                out=grouped[:].rearrange("p (n t) -> p n t", t=4)[:, BLOCK // 2 : BLOCK, :],
-                in0=c_planes[b][:].rearrange("p t n -> p n t")[:, BLOCK // 2 : BLOCK, :],
+                out=words[:, half:BLOCK, :], in0=planes[:, half:BLOCK, :],
                 scalar1=1.0, scalar2=0.0, op0=MULT, op1=ADD,
             )
             c_grouped[b] = grouped

from contextlib import ExitStack

import concourse.mybir as mybir
from concourse.masks import make_identity

F32 = mybir.dt.float32
BF16 = mybir.dt.bfloat16
U32 = mybir.dt.uint32
U8 = mybir.dt.uint8
FP8X4 = mybir.dt.float8_e4m3fn_x4
ADD = mybir.AluOpType.add
MULT = mybir.AluOpType.mult
IDENTITY = mybir.ActivationFunctionType.Identity

P = 128
TOKENS = 4096
K = 512
HEADS = 6
HEAD = 128
HALF = HEAD // 2
E = HEADS * HEAD
T_HEADS = 5
BANK = 512
TILES = TOKENS // P
BLOCK_TILES = 4
BLOCK = BLOCK_TILES * P
BLOCKS = TILES // BLOCK_TILES
BLOCK_OUT = BLOCK_TILES * E

BY_SCALAR = (1, 4)

FLOPS = 2 * TOKENS * K * (K + 2 * E)


def tile_selfattention_pa_t_kernel(
    tc, x, rope_cos, rope_sin, wkv_down, bkv_down, wk_up, bk_up, wv_up, bv_up, out_0, out_1
):
    nc = tc.nc
    with ExitStack() as stack:
        consts = stack.enter_context(tc.tile_pool(name="consts", bufs=1))
        rows = stack.enter_context(tc.tile_pool(name="rows", bufs=1))
        weights = stack.enter_context(tc.tile_pool(name="weights", bufs=1))
        x_stage = stack.enter_context(tc.tile_pool(name="x_stage", bufs=3))
        c_stage = stack.enter_context(tc.tile_pool(name="c_stage", bufs=2))
        pairs = stack.enter_context(tc.tile_pool(name="pairs", bufs=2))
        triples = stack.enter_context(tc.tile_pool(name="triples", bufs=3))
        s_banks = stack.enter_context(tc.psum_pool(name="s_banks", bufs=3))
        v_banks = stack.enter_context(tc.psum_pool(name="v_banks", bufs=5))
        stack.enter_context(tc.manual_schedule())

        x_dram = x.rearrange("(p t) d -> p t d", t=TILES)
        cos_dram = rope_cos.rearrange("(p t) j -> p t j", t=TILES)
        sin_dram = rope_sin.rearrange("(p t) j -> p t j", t=TILES)
        k_dram = out_0.rearrange("(p t) h j -> p t (h j)", t=TILES)
        v_dram = out_1.rearrange("(p t) h j -> p (t h j)", t=TILES)

        x_rows = rows.tile([P, TILES, K], BF16)
        cos_rows = rows.tile([P, TILES, HEAD], BF16)
        sin_rows = rows.tile([P, TILES, HEAD], BF16)
        sin_rot = rows.tile([P, TILES, HEAD], BF16)
        down_rows = rows.tile([P, 4, K], BF16)
        up_rows = rows.tile([P, 2 * HEADS, K], BF16)
        bkv_bf = consts.tile([P, 4], BF16)
        bk_bf = consts.tile([P, T_HEADS], BF16)
        bk_row = consts.tile([P, HEAD], BF16)
        bv_row = consts.tile([P, 2, E], BF16)

        def tiles_of(b):
            return slice(b * BLOCK_TILES, (b + 1) * BLOCK_TILES)

        def load_x(b):
            nc.sync.dma_start(out=x_rows[:, tiles_of(b), :], in_=x_dram[:, tiles_of(b), :])

        def load_rope(b):
            nc.sync.dma_start(out=cos_rows[:, tiles_of(b), :], in_=cos_dram[:, tiles_of(b), :])
            nc.sync.dma_start(out=sin_rows[:, tiles_of(b), :], in_=sin_dram[:, tiles_of(b), :])

        nc.sync.dma_start(out=down_rows[:], in_=wkv_down.rearrange("(m t) d -> m t d", t=4))
        load_x(0)
        nc.sync.dma_start(out=bkv_bf[:], in_=bkv_down.rearrange("(m t) -> m t", t=4))
        wk_rows = wk_up.rearrange("(a m) c -> m a c", m=P)
        wv_rows = wv_up.rearrange("(a m) c -> m a c", m=P)
        nc.sync.dma_start(out=up_rows[:, 4:HEADS, :], in_=wk_rows[:, 4:HEADS, :])
        nc.sync.dma_start(out=up_rows[:, HEADS : HEADS + 2, :], in_=wv_rows[:, 0:2, :])
        nc.sync.dma_start(out=up_rows[:, HEADS + 2 : 2 * HEADS, :], in_=wv_rows[:, 2:HEADS, :])
        load_x(1)
        nc.sync.dma_start(out=bk_row[:], in_=bk_up[T_HEADS * HEAD : E].partition_broadcast(P))
        nc.sync.dma_start(out=bv_row[:, 0, :], in_=bv_up.partition_broadcast(P))
        with nc.allow_non_contiguous_dma(reason="640 bias values, one head to a column"):
            nc.sync.dma_start(out=bk_bf[:], in_=bk_up[0 : T_HEADS * HEAD].rearrange("(h m) -> m h", m=P))
        load_rope(0)
        nc.sync.dma_start(out=up_rows[:, 0:4, :], in_=wk_rows[:, 0:4, :])
        for b in range(2, BLOCKS):
            load_x(b)
            load_rope(b - 1)
        load_rope(BLOCKS - 1)

        ident_f32 = consts.tile([P, P], F32)
        make_identity(nc, ident_f32[:])
        ident_bf = consts.tile([P, P], BF16)
        make_identity(nc, ident_bf[:])
        swap_f32 = consts.tile([P, P], F32)
        nc.vector.tensor_copy(out=swap_f32[:, 0:HALF], in_=ident_f32[:, HALF:HEAD])
        nc.vector.tensor_copy(out=swap_f32[:, HALF:HEAD], in_=ident_f32[:, 0:HALF])
        bkv_col = consts.tile([P, 4], F32)
        bk_col = consts.tile([P, T_HEADS], F32)

        def rotate_sin(b):
            nc.gpsimd.tensor_scalar(
                out=sin_rot[:, tiles_of(b), 0:HALF], in0=sin_rows[:, tiles_of(b), HALF:HEAD],
                scalar1=1.0, scalar2=0.0, op0=MULT, op1=ADD,
            )
            nc.gpsimd.tensor_scalar(
                out=sin_rot[:, tiles_of(b), HALF:HEAD], in0=sin_rows[:, tiles_of(b), 0:HALF],
                scalar1=-1.0, scalar2=0.0, op0=MULT, op1=ADD,
            )

        down_codes = weights.tile([P, K], U32, align_bytes=64)
        down_scales = weights.tile([P, K], U8, align_bytes=64)
        up_codes = weights.tile([P, 2 * E], U32, align_bytes=64)
        up_scales = weights.tile([P, 2 * E], U8, align_bytes=64)

        def words_to_partitions(four_tiles, banks, copy):
            grouped = x_stage.tile([P, 4 * BLOCK], BF16, align_bytes=64)
            words_in = four_tiles.bitcast(F32)
            words_out = grouped[:].bitcast(F32).rearrange("p (r n u) -> p r n u", r=4, u=2)
            for first in (0, 2):
                bank = banks.tile([P, 2, 2, P], F32, tag="bank")
                for r in range(2):
                    for u in range(2):
                        nc.tensor.transpose(
                            bank[:, r, u, :], words_in[:, first + r, u : 2 * P : 2], ident_f32[:]
                        )
                copy(
                    out=words_out[:, first : first + 2, :, :],
                    in_=bank[:].rearrange("p r u n -> p r n u"),
                )
            return grouped

        def quantise(grouped, codes, scales):
            nc.vector.quantize_mx(out=codes.bitcast(FP8X4), scales=scales, in_=grouped[:])

        x_grouped = {}
        x_mx = {}
        c_planes = {}
        c_grouped = {}
        c_mx = {}
        tables = {}
        products = {}
        k_banks = {}
        k_outs = {}
        k_in = {}
        v_outs = {}

        def x_words(b):
            x_grouped[b] = words_to_partitions(x_rows[:, tiles_of(b), :], s_banks, nc.scalar.copy)

        def x_quantise(b):
            x_codes = pairs.tile([P, BLOCK], U32, align_bytes=64)
            x_scales = pairs.tile([P, BLOCK], U8, align_bytes=64)
            quantise(x_grouped[b], x_codes[:], x_scales[:])
            x_mx[b] = (x_codes, x_scales)

        def ckv_matmuls(b, parts=range(4)):
            x_codes, x_scales = x_mx[b]
            if b not in c_planes:
                planes = pairs.tile([P, 4, BLOCK], BF16)
                c_planes[b] = planes
            planes = c_planes[b]
            for t in parts:
                cols = slice(t * P, (t + 1) * P)
                bank = s_banks.tile([P, BLOCK], F32, tag="bank")
                nc.tensor.matmul_mx(
                    out=bank[:],
                    lhsT=down_codes[:, cols].bitcast(FP8X4),
                    lhsT_scale=down_scales[:, cols],
                    rhs=x_codes[:].bitcast(FP8X4),
                    rhs_scale=x_scales[:],
                    start=True,
                    stop=True,
                )
                nc.scalar.activation(
                    out=planes[:, t, :], in_=bank[:], func=IDENTITY, bias=bkv_col[:, t : t + 1], scale=1.0
                )

        def ckv_direct(b):
            x_codes, x_scales = x_mx[b]
            grouped = c_stage.tile([P, 4 * BLOCK], BF16, align_bytes=64)
            for i in range(BLOCK_TILES):
                toks = slice(i * P, (i + 1) * P)
                bank = v_banks.tile([P, 4, P], F32, tag="bank")
                for t in range(4):
                    cols = slice(t * P, (t + 1) * P)
                    nc.tensor.matmul_mx(
                        out=bank[:, t, :],
                        lhsT=down_codes[:, cols].bitcast(FP8X4),
                        lhsT_scale=down_scales[:, cols],
                        rhs=x_codes[:, toks].bitcast(FP8X4),
                        rhs_scale=x_scales[:, toks],
                        start=True,
                        stop=True,
                    )
                nc.vector.tensor_tensor(
                    out=grouped[:, 4 * i * P : 4 * (i + 1) * P].rearrange("p (n t) -> p n t", t=4),
                    in0=bank[:].rearrange("p t n -> p n t"),
                    in1=bkv_col[:].unsqueeze(1).to_broadcast([P, P, 4]),
                    op=ADD,
                )
            c_grouped[b] = grouped

        def ckv_regroup(b):
            grouped = c_stage.tile([P, 4 * BLOCK], BF16, align_bytes=64)
            words = grouped[:].rearrange("p (n t) -> p n t", t=4)
            planes = c_planes[b][:].rearrange("p t n -> p n t")
            half = BLOCK // 2
            nc.scalar.copy(out=words[:, 0:half, :], in_=planes[:, 0:half, :])
            nc.gpsimd.tensor_scalar(
                out=words[:, half:BLOCK, :], in0=planes[:, half:BLOCK, :],
                scalar1=1.0, scalar2=0.0, op0=MULT, op1=ADD,
            )
            c_grouped[b] = grouped

        def ckv_quantise(b):
            c_codes = pairs.tile([P, BLOCK], U32, align_bytes=64)
            c_scales = pairs.tile([P, BLOCK], U8, align_bytes=64)
            quantise(c_grouped[b], c_codes[:], c_scales[:])
            c_mx[b] = (c_codes, c_scales)

        def rope_tables(b):
            bank = s_banks.tile([P, 2, BLOCK_TILES, P], BF16, tag="bank")
            for i in range(BLOCK_TILES):
                nc.tensor.transpose(bank[:, 0, i, :], cos_rows[:, b * BLOCK_TILES + i, :], ident_bf[:])
                nc.tensor.transpose(bank[:, 1, i, :], sin_rot[:, b * BLOCK_TILES + i, :], ident_bf[:])
            table = pairs.tile([P, 2, BLOCK], BF16)
            nc.scalar.copy(out=table[:], in_=bank[:].rearrange("p w i n -> p w (i n)"))
            tables[b] = table

        def k_matmuls(b):
            c_codes, c_scales = c_mx[b]
            k_banks[b] = []
            for h in range(T_HEADS):
                cols = slice(h * HEAD, (h + 1) * HEAD)
                bank = v_banks.tile([P, BLOCK], F32, tag="bank")
                nc.tensor.matmul_mx(
                    out=bank[:],
                    lhsT=up_codes[:, cols].bitcast(FP8X4),
                    lhsT_scale=up_scales[:, cols],
                    rhs=c_codes[:].bitcast(FP8X4),
                    rhs_scale=c_scales[:],
                    start=True,
                    stop=True,
                )
                k_banks[b].append(bank)

        def k_products(b, heads=range(T_HEADS)):
            if b not in products:
                product = pairs.tile([P, T_HEADS, 2, BLOCK], F32)
                products[b] = product
            product = products[b]
            for h in heads:
                nc.vector.scalar_tensor_tensor(
                    out=product[:, h, :, :],
                    in0=k_banks[b][h][:].unsqueeze(1).to_broadcast([P, 2, BLOCK]),
                    scalar=bk_col[:, h : h + 1],
                    in1=tables[b][:],
                    op0=ADD,
                    op1=MULT,
                )

        def k_back(b, heads=range(T_HEADS)):
            product = products[b]
            k_out = k_outs[b]
            for h in heads:
                bank = s_banks.tile([P, BLOCK_TILES, HEAD], F32, tag="bank")
                for i in range(BLOCK_TILES):
                    toks = slice(i * P, (i + 1) * P)
                    nc.tensor.matmul(
                        out=bank[:, i, :], lhsT=product[:, h, 0, toks], rhs=ident_f32[:],
                        is_transpose=True, start=True, stop=False,
                    )
                    nc.tensor.matmul(
                        out=bank[:, i, :], lhsT=product[:, h, 1, toks], rhs=swap_f32[:],
                        is_transpose=True, start=False, stop=True,
                    )
                nc.scalar.copy(out=k_out[:, :, h, :], in_=bank[:])

        def k_store(b, heads=range(HEADS)):
            cols = slice(heads[0] * HEAD, (heads[-1] + 1) * HEAD)
            nc.sync.dma_start(
                out=k_dram[:, tiles_of(b), cols],
                in_=k_outs[b][:].rearrange("p i h j -> p i (h j)")[:, :, cols],
            )

        def k_rows(b):
            c_codes, c_scales = c_mx[b]
            w_cols = slice(T_HEADS * HEAD, E)
            bank = v_banks.tile([P, BLOCK_TILES, HEAD], F32, tag="bank")
            for i in range(BLOCK_TILES):
                toks = slice(i * P, (i + 1) * P)
                nc.tensor.matmul_mx(
                    out=bank[:, i, :],
                    lhsT=c_codes[:, toks].bitcast(FP8X4),
                    lhsT_scale=c_scales[:, toks],
                    rhs=up_codes[:, w_cols].bitcast(FP8X4),
                    rhs_scale=up_scales[:, w_cols],
                    start=True,
                    stop=True,
                )
            k_row = pairs.tile([P, BLOCK_TILES, HEAD], F32)
            nc.vector.tensor_tensor(
                out=k_row[:], in0=bank[:], in1=bk_row[:].unsqueeze(1).to_broadcast([P, BLOCK_TILES, HEAD]), op=ADD
            )
            k_in[b] = k_row

        def rope_rows(b):
            k_out = triples.tile([P, BLOCK_TILES, HEADS, HEAD], F32)
            k_outs[b] = k_out
            k_row = k_in[b]
            out = k_out[:, :, T_HEADS, :]
            nc.gpsimd.tensor_tensor(out=out, in0=k_row[:], in1=cos_rows[:, tiles_of(b), :], op=MULT)
            nc.gpsimd.tensor_tensor(out=k_row[:], in0=k_row[:], in1=sin_rot[:, tiles_of(b), :], op=MULT)
            nc.gpsimd.tensor_tensor(
                out=out[:, :, 0:HALF], in0=out[:, :, 0:HALF], in1=k_row[:, :, HALF:HEAD], op=ADD
            )
            nc.gpsimd.tensor_tensor(
                out=out[:, :, HALF:HEAD], in0=out[:, :, HALF:HEAD], in1=k_row[:, :, 0:HALF], op=ADD
            )

        def v_banks_of(b, banks_here):
            c_codes, c_scales = c_mx[b]
            if b not in v_outs:
                v_out = pairs.tile([P, BLOCK_OUT], F32)
                v_outs[b] = v_out
            v_out = v_outs[b]
            bias = bv_row[:].rearrange("p r e -> p (r e)")
            for q in banks_here:
                by_scalar = q in BY_SCALAR and b < BLOCKS - 1
                bank = (s_banks if by_scalar else v_banks).tile([P, BANK], F32, tag="bank")
                col = q * BANK
                while col < (q + 1) * BANK:
                    i, e0 = divmod(col, E)
                    width = min(E - e0, (q + 1) * BANK - col)
                    toks = slice(i * P, (i + 1) * P)
                    w_cols = slice(E + e0, E + e0 + width)
                    nc.tensor.matmul_mx(
                        out=bank[:, col - q * BANK : col - q * BANK + width],
                        lhsT=c_codes[:, toks].bitcast(FP8X4),
                        lhsT_scale=c_scales[:, toks],
                        rhs=up_codes[:, w_cols].bitcast(FP8X4),
                        rhs_scale=up_scales[:, w_cols],
                        start=True,
                        stop=True,
                    )
                    col += width
                o_cols = slice(q * BANK, (q + 1) * BANK)
                first = q * BANK % E
                b_cols = slice(first, first + BANK)
                if by_scalar:
                    nc.scalar.copy(out=v_out[:, o_cols], in_=bank[:])
                    nc.gpsimd.tensor_tensor(out=v_out[:, o_cols], in0=v_out[:, o_cols], in1=bias[:, b_cols], op=ADD)
                else:
                    nc.vector.tensor_tensor(out=v_out[:, o_cols], in0=bank[:], in1=bias[:, b_cols], op=ADD)

        def v_store(b, half):
            cols = slice(half * BLOCK_OUT // 2, (half + 1) * BLOCK_OUT // 2)
            nc.sync.dma_start(
                out=v_dram[:, b * BLOCK_OUT + cols.start : b * BLOCK_OUT + cols.stop], in_=v_outs[b][:, cols]
            )

        def down_weights():
            grouped = words_to_partitions(down_rows[:], v_banks, nc.vector.tensor_copy)
            quantise(grouped, down_codes[:], down_scales[:])
            nc.vector.tensor_copy(out=bkv_col[:], in_=bkv_bf[:])

        up_grouped = {}

        def up_words(chunk):
            rows_here = up_rows[:, 4 * chunk : 4 * chunk + 4, :]
            up_grouped[chunk] = words_to_partitions(rows_here, s_banks, nc.scalar.copy)

        def up_quantise(chunk):
            cols = slice(chunk * BLOCK, (chunk + 1) * BLOCK)
            quantise(up_grouped[chunk], up_codes[:, cols], up_scales[:, cols])

        down_weights()
        x_words(0)
        up_words(1)
        rotate_sin(0)
        x_quantise(0)
        up_quantise(1)
        ckv_direct(0)
        up_words(2)
        ckv_quantise(0)
        x_words(1)
        up_quantise(2)
        x_quantise(1)
        nc.gpsimd.tensor_scalar(
            out=bv_row[:, 1, :], in0=bv_row[:, 0, :], scalar1=1.0, scalar2=0.0, op0=MULT, op1=ADD
        )
        k_rows(0)
        rope_rows(0)
        for q in (0, 2, 3, 5):
            v_banks_of(0, [q])
        rotate_sin(1)
        up_words(0)
        up_quantise(0)
        rope_tables(0)
        ckv_direct(1)
        x_words(2)
        nc.vector.tensor_copy(out=bk_col[:], in_=bk_bf[:])
        k_matmuls(0)
        v_banks_of(0, [4])
        x_words(3)
        v_banks_of(0, [1])
        v_store(0, 0)
        v_store(0, 1)
        x_quantise(2)
        k_products(0, [0])
        ckv_matmuls(2, [0, 1])
        k_products(0, [1])
        ckv_quantise(1)
        ckv_matmuls(2, [2, 3])
        k_products(0, [2])
        x_quantise(3)
        rotate_sin(2)
        ckv_regroup(2)
        rope_tables(1)
        k_products(0, [3, 4])
        ckv_quantise(2)

        for b in range(1, BLOCKS - 1):
            v_banks_of(b, [1])
            k_rows(b)
            v_banks_of(b, [0])
            if b + 2 < BLOCKS:
                ckv_matmuls(b + 2, [0, 1])
            rope_rows(b)
            v_banks_of(b, [2])
            v_store(b, 0)
            v_banks_of(b, [3])
            if b + 2 < BLOCKS:
                ckv_matmuls(b + 2, [2])
            v_banks_of(b, [5])
            if b + 2 < BLOCKS:
                ckv_matmuls(b + 2, [3])
            v_banks_of(b, [4])
            v_store(b, 1)
            k_matmuls(b)
            if b + 2 < BLOCKS:
                ckv_regroup(b + 2)
            k_products(b)
            if b + 2 < BLOCKS:
                rotate_sin(b + 2)
            if b + 3 < BLOCKS:
                x_words(b + 3)
            k_back(b - 1, [0])
            rope_tables(b + 1)
            k_back(b - 1, [1, 2, 3, 4])
            k_store(b - 1)
            if b + 3 < BLOCKS:
                x_quantise(b + 3)
            if b + 2 < BLOCKS:
                ckv_quantise(b + 2)

        last = BLOCKS - 1
        for q in range(6):
            v_banks_of(last, [q])
        v_store(last, 0)
        v_store(last, 1)
        k_rows(last)
        rope_rows(last)
        k_back(last - 1, [0, 1, 2])
        k_matmuls(last)
        k_back(last - 1, [3, 4])
        k_store(last - 1)
        k_products(last, [0, 1])
        k_back(last, [0, 1])
        k_store(last, range(0, 2))
        k_products(last, [2, 3, 4])
        k_back(last, [2, 3, 4])
        k_store(last, range(2, HEADS))
